import numpy as np
import ml_dtypes


def mxq(x, axis, fmt="e4m3"):
    dtype, down = {"e4m3": (ml_dtypes.float8_e4m3fn, 7), "e5m2": (ml_dtypes.float8_e5m2, 14)}[fmt]
    v = np.moveaxis(np.asarray(x, np.float32).astype(ml_dtypes.bfloat16).astype(np.float64), axis, -1)
    blocks = v.reshape(v.shape[:-1] + (-1, 32))
    amax = np.abs(blocks).max(-1, keepdims=True)
    byte = np.maximum(np.where(amax > 0, np.frexp(amax)[1] - 1 + 127, 0) - down, 1)
    scale = np.exp2(byte - 127.0)
    codes = (blocks / scale).astype(np.float32).astype(dtype).astype(np.float64)
    return np.moveaxis((codes * scale).reshape(v.shape), -1, axis)


WIDE = False


def mx_kscale(k):
    if not WIDE:
        return np.ones(k)
    levels = np.array([10, -10, 5, -5, 0])
    a = np.random.permutation(np.resize(levels, k // 512 * 4)).reshape(k // 512, 4)
    idx = np.arange(k)
    return np.exp2(a[idx // 512, idx % 128 // 32])


BF16 = ml_dtypes.bfloat16


def bf(x):
    return np.asarray(x, np.float32).astype(BF16)


def f64(x):
    return np.asarray(x).astype(np.float64)


B, H0, C0, C1, C2, NA, NO = 2, 32, 512, 16384, 1024, 3, 128
H1, H2 = H0 // 2, H0 // 4
O = NA * NO


def sigmoid(v):
    return 1.0 / (1.0 + np.exp(-v))


def _draw_level(c, h):
    s = mx_kscale(c)
    f = bf(np.random.standard_normal((B, c, h, h)) * s[None, :, None, None])
    w = bf(np.random.standard_normal((O, c)) / np.sqrt(c) / s[None, :])
    b = bf(np.random.standard_normal(O) * 0.5)
    return f, w, b


def setup_inputs():
    f0, w0, b0 = _draw_level(C0, H0)
    f1, w1, b1 = _draw_level(C1, H1)
    f2, w2, b2 = _draw_level(C2, H2)
    anchors = bf(1.0 + 4.0 * np.random.random((3, NA, 2)))
    return {"f0": f0, "f1": f1, "f2": f2, "w0": w0, "b0": b0, "w1": w1, "b1": b1, "w2": w2, "b2": b2, "anchors": anchors}


def _decode_level(f, w, b, anchors_i):
    nb, c, h, wd = f.shape
    y = (mxq(w, 1, "e4m3") @ mxq(f.reshape(nb, c, h * wd), 1, "e4m3")) + b[None, :, None]
    y = y.reshape(nb, NA, NO, h, wd).transpose(0, 1, 3, 4, 2)
    xy = 2.0 * sigmoid(y[..., 0:2]) - 0.5
    wh = np.square(2.0 * sigmoid(y[..., 2:4])) * anchors_i[None, :, None, None, :]
    rest = y[..., 4:]
    out = np.concatenate([xy, wh, rest], axis=-1)
    return out.reshape(nb, -1, NO)


def reference(f0, f1, f2, w0, b0, w1, b1, w2, b2, anchors):
    a = f64(anchors)
    outs = [
        _decode_level(f64(f0), f64(w0), f64(b0), a[0]),
        _decode_level(f64(f1), f64(w1), f64(b1), a[1]),
        _decode_level(f64(f2), f64(w2), f64(b2), a[2]),
    ]
    return np.concatenate(outs, axis=1)

@@ -1,0 +1,258 @@
+from contextlib import ExitStack
+
+import concourse.mybir as mybir
+from concourse.masks import make_identity
+
+BF16 = mybir.dt.bfloat16
+F32 = mybir.dt.float32
+U32 = mybir.dt.uint32
+U8 = mybir.dt.uint8
+FP8X4 = mybir.dt.float8_e4m3fn_x4
+ADD = mybir.AluOpType.add
+MULT = mybir.AluOpType.mult
+SIGMOID = mybir.ActivationFunctionType.Sigmoid
+
+P = 128
+PACK = 4
+K_PASS = P * PACK
+IMAGES = 2
+ANCHORS = 3
+FIELDS = 128
+BANK = 512
+CHUNK_PASSES = 4
+BANK_PASSES = 2
+UNIT_PIXELS = 256
+RUN = 4
+RAW_CHUNKS = 3
+LOADS_AHEAD = 2
+
+FLOPS = 2 * ANCHORS * FIELDS * IMAGES * (512 * 1024 + 16384 * 256 + 1024 * 64)
+
+
+def tile_head_k_kernel(tc, f0, f1, f2, w0, b0, w1, b1, w2, b2, anchors, out):
+    nc = tc.nc
+
+    level0 = dict(index=0, f=f0, w=w0, first_row=0, weights_stationary=False)
+    level1 = dict(index=1, f=f1, w=w1, first_row=3072, weights_stationary=True)
+    level2 = dict(index=2, f=f2, w=w2, first_row=3840, weights_stationary=False)
+    chunks = []
+    for level in (level0, level2, level1):
+        level["pixels"] = level["f"].shape[2] * level["f"].shape[3]
+        level["passes"] = level["w"].shape[1] // K_PASS
+        for first_pass in range(0, level["passes"], CHUNK_PASSES):
+            passes = min(CHUNK_PASSES, level["passes"] - first_pass)
+            chunks.append(dict(level=level, first_pass=first_pass, passes=passes))
+
+    with ExitStack() as ctx:
+        ctx.enter_context(tc.manual_schedule())
+        consts = ctx.enter_context(tc.tile_pool(name="consts", bufs=1))
+        stream = ctx.enter_context(tc.tile_pool(name="stream", bufs=2))
+        psum = ctx.enter_context(tc.psum_pool(name="psum", bufs=4))
+
+        identity = consts.tile([P, P], F32)
+        make_identity(nc, identity[:])
+
+        ones = consts.tile([P, P], BF16)
+        nc.vector.memset(ones[:], 1.0)
+        row0 = consts.tile([P, 3, BANK], BF16)
+        nc.vector.memset(row0[:], 0.0)
+        outputs = ANCHORS * FIELDS
+        for i, b in enumerate((b0, b1, b2)):
+            nc.scalar.dma_start(out=row0[0:1, i, 0:outputs], in_=b.rearrange("(x o) -> x o", x=1))
+        nc.scalar.dma_start(
+            out=row0[0:1, :, outputs : outputs + 2 * ANCHORS],
+            in_=anchors.rearrange("(x l) a s -> x l (a s)", x=1),
+        )
+        spread = consts.tile([P, 3, BANK], F32)
+        for i in range(3):
+            spread_ps = psum.tile([P, BANK], F32, tag="y")
+            nc.tensor.matmul(out=spread_ps[:], lhsT=ones[:], rhs=row0[:, i, :], start=True, stop=True)
+            nc.vector.tensor_copy(out=spread[:, i, :], in_=spread_ps[:])
+        four_anchors = spread[:, :, outputs : outputs + 2 * ANCHORS]
+        nc.vector.tensor_scalar(out=four_anchors, in0=four_anchors, scalar1=4.0, scalar2=None, op0=MULT)
+
+        def load(chunk):
+            level = chunk["level"]
+            k0 = chunk["first_pass"] * K_PASS
+            k1 = k0 + chunk["passes"] * K_PASS
+            w_raw = stream.tile([P, ANCHORS, k1 - k0], BF16, tag="w_raw", bufs=RAW_CHUNKS, name="w_raw")
+            nc.sync.dma_start(out=w_raw[:], in_=level["w"][:, k0:k1].rearrange("(a o) k -> o a k", a=ANCHORS))
+            chunk["w_raw"] = w_raw
+            chunk["f_raw"] = []
+            for n in range(IMAGES):
+                f_raw = stream.tile(
+                    [P, chunk["passes"], PACK, level["pixels"]],
+                    BF16,
+                    tag="f_raw",
+                    bufs=IMAGES * RAW_CHUNKS,
+                    name="f_raw",
+                )
+                nc.sync.dma_start(
+                    out=f_raw[:],
+                    in_=level["f"][n, k0:k1].rearrange("(g p t) h w -> p g t (h w)", p=P, t=PACK),
+                )
+                chunk["f_raw"].append(f_raw)
+
+        def transpose_weights(chunk):
+            w_words = chunk["w_raw"][:].bitcast(F32).rearrange("o a (g p u) -> o a g u p", p=P, u=2)
+            chunk["w_grouped"] = []
+            for a in range(ANCHORS):
+                w_grouped = stream.tile(
+                    [P, chunk["passes"], FIELDS, PACK], BF16, tag="w_grouped", bufs=4, align_bytes=64, name="w_grouped"
+                )
+                grouped_words = w_grouped[:].bitcast(F32)
+                for g0 in range(0, chunk["passes"], BANK_PASSES):
+                    count = min(BANK_PASSES, chunk["passes"] - g0)
+                    w_t = psum.tile([P, count, 2, FIELDS], F32, tag="w_t", name="w_t")
+                    for g in range(count):
+                        for u in range(2):
+                            nc.tensor.transpose(out=w_t[:, g, u, :], in_=w_words[:, a, g0 + g, u, :], identity=identity[:])
+                    nc.scalar.copy(out=grouped_words[:, g0 : g0 + count], in_=w_t[:].rearrange("p g u o -> p g o u"))
+                chunk["w_grouped"].append(w_grouped)
+
+        def regroup(copy, chunk, unit):
+            g, n, x0, width = unit
+            f_grouped = stream.tile([P, width, PACK], BF16, tag="f_grouped", bufs=8, align_bytes=64, name="f_grouped")
+            copy(
+                out=f_grouped[:].rearrange("p (c i) t -> p c t i", i=RUN),
+                in_=chunk["f_raw"][n][:, g, :, x0 : x0 + width].rearrange("p t (c i) -> p c t i", i=RUN),
+            )
+            return f_grouped
+
+        def quantise_features(chunk, unit, f_grouped):
+            g, n, x0, width = unit
+            first = n * chunk["level"]["pixels"] + x0
+            nc.vector.quantize_mx(
+                out=chunk["f_codes"][:, g, first : first + width].bitcast(FP8X4),
+                scales=chunk["f_scales"][:, g, first : first + width],
+                in_=f_grouped[:].rearrange("p x t -> p (x t)"),
+            )
+
+        def quantise(chunk):
+            passes = chunk["passes"]
+            pixels = chunk["level"]["pixels"]
+            chunk["f_codes"] = stream.tile([P, passes, IMAGES * pixels], U32, tag="f_codes", align_bytes=64, name="f_codes")
+            chunk["f_scales"] = stream.tile([P, passes, IMAGES * pixels], U8, tag="f_scales", align_bytes=64, name="f_scales")
+            chunk["w_codes"] = stream.tile([P, ANCHORS, passes, FIELDS], U32, tag="w_codes", align_bytes=64, name="w_codes")
+            chunk["w_scales"] = stream.tile([P, ANCHORS, passes, FIELDS], U8, tag="w_scales", align_bytes=64, name="w_scales")
+            width = min(pixels, UNIT_PIXELS)
+            units = [(g, n, x0, width) for g in range(passes) for n in range(IMAGES) for x0 in range(0, pixels, width)]
+            split = len(units) * 5 // 8
+            scalar_tiles = [regroup(nc.scalar.copy, chunk, unit) for unit in units[split:]]
+            waiting = None
+            for unit in units[:split]:
+                f_grouped = regroup(nc.vector.tensor_copy, chunk, unit)
+                if waiting is not None:
+                    quantise_features(chunk, waiting[0], waiting[1])
+                waiting = (unit, f_grouped)
+            quantise_features(chunk, waiting[0], waiting[1])
+            for a in range(ANCHORS):
+                nc.vector.quantize_mx(
+                    out=chunk["w_codes"][:, a].rearrange("p g o -> p (g o)").bitcast(FP8X4),
+                    scales=chunk["w_scales"][:, a].rearrange("p g o -> p (g o)"),
+                    in_=chunk["w_grouped"][a][:].rearrange("p g o t -> p (g o t)"),
+                )
+            for unit, f_grouped in zip(units[split:], scalar_tiles):
+                quantise_features(chunk, unit, f_grouped)
+
+        def add_bias(level, y, t):
+            bias = spread[:, level["index"], 0:outputs].rearrange("p (a j) -> p a j", a=ANCHORS)
+            nc.vector.tensor_tensor(out=level["staged"][:, t], in0=y[:], in1=bias, op=ADD)
+
+        def multiply(chunk):
+            level = chunk["level"]
+            if chunk["first_pass"] == 0:
+                tiles = IMAGES * level["pixels"] // P
+                level["staged"] = consts.tile([P, tiles, ANCHORS, FIELDS], F32, name="staged%d" % level["index"])
+            if level["weights_stationary"]:
+                if chunk["first_pass"] == 0:
+                    level["sums"] = [psum.tile([P, BANK], F32, tag="y", name="sums%d" % a) for a in range(ANCHORS)]
+                for g in range(chunk["passes"]):
+                    k_pass = chunk["first_pass"] + g
+                    for a in range(ANCHORS):
+                        nc.tensor.matmul_mx(
+                            out=level["sums"][a][:],
+                            lhsT=chunk["w_codes"][:, a, g, :].bitcast(FP8X4),
+                            lhsT_scale=chunk["w_scales"][:, a, g, :],
+                            rhs=chunk["f_codes"][:, g, :].bitcast(FP8X4),
+                            rhs_scale=chunk["f_scales"][:, g, :],
+                            start=(k_pass == 0),
+                            stop=(k_pass == level["passes"] - 1),
+                        )
+            else:
+                for t in range(IMAGES * level["pixels"] // P):
+                    y = psum.tile([P, ANCHORS, FIELDS], F32, tag="y", name="y")
+                    for a in range(ANCHORS):
+                        for g in range(chunk["passes"]):
+                            nc.tensor.matmul_mx(
+                                out=y[:, a, :],
+                                lhsT=chunk["f_codes"][:, g, t * P : (t + 1) * P].bitcast(FP8X4),
+                                lhsT_scale=chunk["f_scales"][:, g, t * P : (t + 1) * P],
+                                rhs=chunk["w_codes"][:, a, g, :].bitcast(FP8X4),
+                                rhs_scale=chunk["w_scales"][:, a, g, :],
+                                start=(g == 0),
+                                stop=(g == chunk["passes"] - 1),
+                            )
+                    add_bias(level, y, t)
+
+        def turn_sums(level):
+            by_field = consts.tile([P, ANCHORS, BANK], F32)
+            for a in range(ANCHORS):
+                copy = nc.vector.tensor_copy if a % 2 else nc.scalar.copy
+                copy(out=by_field[:, a, :], in_=level["sums"][a][:])
+            for t in range(IMAGES * level["pixels"] // P):
+                y = psum.tile([P, ANCHORS, FIELDS], F32, tag="y", name="y")
+                for a in range(ANCHORS):
+                    nc.tensor.transpose(out=y[:, a, :], in_=by_field[:, a, t * P : (t + 1) * P], identity=identity[:])
+                add_bias(level, y, t)
+
+        def decode_and_store(level, queue):
+            i = level["index"]
+            pixels = level["pixels"]
+            tiles = IMAGES * pixels // P
+            staged = level["staged"]
+            rows = staged[:].rearrange("p t a j -> p (t a) j")
+            sig = consts.tile([P, tiles * ANCHORS, 4], F32, name="sig%d" % i)
+            nc.scalar.activation(out=sig[:], in_=rows[:, :, 0:4], func=SIGMOID)
+            nc.vector.tensor_scalar(out=rows[:, :, 0:2], in0=sig[:, :, 0:2], scalar1=2.0, scalar2=-0.5, op0=MULT, op1=ADD)
+            squares = consts.tile([P, tiles, ANCHORS, 2], F32, name="squares%d" % i)
+            nc.vector.tensor_tensor(
+                out=squares[:].rearrange("p t a s -> p (t a) s"), in0=sig[:, :, 2:4], in1=sig[:, :, 2:4], op=MULT
+            )
+            nc.vector.tensor_tensor(
+                out=staged[:, :, :, 2:4],
+                in0=squares[:],
+                in1=four_anchors[:, i, :]
+                .rearrange("p (a s) -> p a s", s=2)
+                .unsqueeze(1)
+                .to_broadcast([P, tiles, ANCHORS, 2]),
+                op=MULT,
+            )
+            height = min(P, pixels)
+            for first in range(0, IMAGES * pixels, height):
+                n, x0 = divmod(first, pixels)
+                t, p0 = divmod(first, P)
+                level_rows = out[n, level["first_row"] : level["first_row"] + ANCHORS * pixels, :]
+                queue.dma_start(
+                    out=level_rows.rearrange("(a x) j -> x a j", a=ANCHORS)[x0 : x0 + height],
+                    in_=staged[p0 : p0 + height, t],
+                )
+
+        for chunk in chunks[:LOADS_AHEAD]:
+            load(chunk)
+        for step in range(len(chunks) + 1):
+            if step + LOADS_AHEAD < len(chunks):
+                load(chunks[step + LOADS_AHEAD])
+            if step < len(chunks):
+                transpose_weights(chunks[step])
+            if step >= 1:
+                multiply(chunks[step - 1])
+            if step < len(chunks):
+                quantise(chunks[step])
+            if step >= 1:
+                done = chunks[step - 1]
+                level = done["level"]
+                if done["first_pass"] + done["passes"] == level["passes"]:
+                    if level["weights_stationary"]:
+                        turn_sums(level)
+                    decode_and_store(level, nc.sync if step == len(chunks) else nc.gpsimd)

@@ -24,7 +24,6 @@ BANK_PASSES = 2
 UNIT_PIXELS = 256
 RUN = 4
 RAW_CHUNKS = 3
-LOADS_AHEAD = 2
 
 FLOPS = 2 * ANCHORS * FIELDS * IMAGES * (512 * 1024 + 16384 * 256 + 1024 * 64)
 
@@ -39,9 +38,14 @@ def tile_head_k_kernel(tc, f0, f1, f2, w0, b0, w1, b1, w2, b2, anchors, out):
     for level in (level0, level2, level1):
         level["pixels"] = level["f"].shape[2] * level["f"].shape[3]
         level["passes"] = level["w"].shape[1] // K_PASS
-        for first_pass in range(0, level["passes"], CHUNK_PASSES):
-            passes = min(CHUNK_PASSES, level["passes"] - first_pass)
+        first_pass = 0
+        while first_pass < level["passes"]:
+            left = level["passes"] - first_pass
+            passes = min(CHUNK_PASSES, left)
+            if level["weights_stationary"] and 1 < left <= CHUNK_PASSES:
+                passes = left // 2
             chunks.append(dict(level=level, first_pass=first_pass, passes=passes))
+            first_pass += passes
 
     with ExitStack() as ctx:
         ctx.enter_context(tc.manual_schedule())
@@ -64,12 +68,17 @@ def tile_head_k_kernel(tc, f0, f1, f2, w0, b0, w1, b1, w2, b2, anchors, out):
             in_=anchors.rearrange("(x l) a s -> x l (a s)", x=1),
         )
         spread = consts.tile([P, 3, BANK], F32)
-        for i in range(3):
-            spread_ps = psum.tile([P, BANK], F32, tag="y")
-            nc.tensor.matmul(out=spread_ps[:], lhsT=ones[:], rhs=row0[:, i, :], start=True, stop=True)
-            nc.vector.tensor_copy(out=spread[:, i, :], in_=spread_ps[:])
         four_anchors = spread[:, :, outputs : outputs + 2 * ANCHORS]
-        nc.vector.tensor_scalar(out=four_anchors, in0=four_anchors, scalar1=4.0, scalar2=None, op0=MULT)
+
+        def spread_constants():
+            for i in range(3):
+                spread_ps = psum.tile([P, BANK], F32, tag="y")
+                nc.tensor.matmul(out=spread_ps[:], lhsT=ones[:], rhs=row0[:, i, :], start=True, stop=True)
+                nc.vector.tensor_copy(out=spread[:, i, :], in_=spread_ps[:])
+            nc.vector.tensor_scalar(out=four_anchors, in0=four_anchors, scalar1=4.0, scalar2=None, op0=MULT)
+
+        table_warmer = consts.tile([P, 1], F32)
+        nc.scalar.activation(out=table_warmer[:], in_=ones[:, 0:1], func=SIGMOID)
 
         def load(chunk):
             level = chunk["level"]
@@ -136,7 +145,7 @@ def tile_head_k_kernel(tc, f0, f1, f2, w0, b0, w1, b1, w2, b2, anchors, out):
             chunk["w_codes"] = stream.tile([P, ANCHORS, passes, FIELDS], U32, tag="w_codes", align_bytes=64, name="w_codes")
             chunk["w_scales"] = stream.tile([P, ANCHORS, passes, FIELDS], U8, tag="w_scales", align_bytes=64, name="w_scales")
             width = min(pixels, UNIT_PIXELS)
-            units = [(g, n, x0, width) for g in range(passes) for n in range(IMAGES) for x0 in range(0, pixels, width)]
+            units = [(g, n, x0, width) for n in range(IMAGES) for g in range(passes) for x0 in range(0, pixels, width)]
             split = len(units) * 5 // 8
             scalar_tiles = [regroup(nc.scalar.copy, chunk, unit) for unit in units[split:]]
             waiting = None
@@ -238,21 +247,24 @@ def tile_head_k_kernel(tc, f0, f1, f2, w0, b0, w1, b1, w2, b2, anchors, out):
                     in_=staged[p0 : p0 + height, t],
                 )
 
-        for chunk in chunks[:LOADS_AHEAD]:
+        def finish(chunk, queue):
+            level = chunk["level"]
+            if chunk["first_pass"] + chunk["passes"] == level["passes"]:
+                if level["weights_stationary"]:
+                    turn_sums(level)
+                decode_and_store(level, queue)
+
+        for chunk in chunks[:RAW_CHUNKS]:
             load(chunk)
-        for step in range(len(chunks) + 1):
-            if step + LOADS_AHEAD < len(chunks):
-                load(chunks[step + LOADS_AHEAD])
-            if step < len(chunks):
-                transpose_weights(chunks[step])
-            if step >= 1:
-                multiply(chunks[step - 1])
-            if step < len(chunks):
-                quantise(chunks[step])
-            if step >= 1:
-                done = chunks[step - 1]
-                level = done["level"]
-                if done["first_pass"] + done["passes"] == level["passes"]:
-                    if level["weights_stationary"]:
-                        turn_sums(level)
-                    decode_and_store(level, nc.sync if step == len(chunks) else nc.gpsimd)
+        transpose_weights(chunks[0])
+        quantise(chunks[0])
+        spread_constants()
+        for step in range(1, len(chunks)):
+            if step + RAW_CHUNKS - 1 < len(chunks):
+                load(chunks[step + RAW_CHUNKS - 1])
+            transpose_weights(chunks[step])
+            multiply(chunks[step - 1])
+            quantise(chunks[step])
+            finish(chunks[step - 1], nc.gpsimd)
+        multiply(chunks[-1])
+        finish(chunks[-1], nc.sync)

@@ -146,7 +146,7 @@ def tile_head_k_kernel(tc, f0, f1, f2, w0, b0, w1, b1, w2, b2, anchors, out):
             chunk["w_scales"] = stream.tile([P, ANCHORS, passes, FIELDS], U8, tag="w_scales", align_bytes=64, name="w_scales")
             width = min(pixels, UNIT_PIXELS)
             units = [(g, n, x0, width) for n in range(IMAGES) for g in range(passes) for x0 in range(0, pixels, width)]
-            split = len(units) * 5 // 8
+            split = len(units) // 2
             scalar_tiles = [regroup(nc.scalar.copy, chunk, unit) for unit in units[split:]]
             waiting = None
             for unit in units[:split]:

@@ -74,7 +74,7 @@ def tile_head_k_kernel(tc, f0, f1, f2, w0, b0, w1, b1, w2, b2, anchors, out):
             for i in range(3):
                 spread_ps = psum.tile([P, BANK], F32, tag="y")
                 nc.tensor.matmul(out=spread_ps[:], lhsT=ones[:], rhs=row0[:, i, :], start=True, stop=True)
-                nc.vector.tensor_copy(out=spread[:, i, :], in_=spread_ps[:])
+                nc.scalar.copy(out=spread[:, i, :], in_=spread_ps[:])
             nc.vector.tensor_scalar(out=four_anchors, in0=four_anchors, scalar1=4.0, scalar2=None, op0=MULT)
 
         table_warmer = consts.tile([P, 1], F32)
@@ -215,7 +215,7 @@ def tile_head_k_kernel(tc, f0, f1, f2, w0, b0, w1, b1, w2, b2, anchors, out):
                     nc.tensor.transpose(out=y[:, a, :], in_=by_field[:, a, t * P : (t + 1) * P], identity=identity[:])
                 add_bias(level, y, t)
 
-        def decode_and_store(level, queue):
+        def decode(level):
             i = level["index"]
             pixels = level["pixels"]
             tiles = IMAGES * pixels // P
@@ -237,22 +237,26 @@ def tile_head_k_kernel(tc, f0, f1, f2, w0, b0, w1, b1, w2, b2, anchors, out):
                 .to_broadcast([P, tiles, ANCHORS, 2]),
                 op=MULT,
             )
+
+        def store(level):
+            pixels = level["pixels"]
+            staged = level["staged"]
             height = min(P, pixels)
             for first in range(0, IMAGES * pixels, height):
                 n, x0 = divmod(first, pixels)
                 t, p0 = divmod(first, P)
                 level_rows = out[n, level["first_row"] : level["first_row"] + ANCHORS * pixels, :]
-                queue.dma_start(
+                nc.sync.dma_start(
                     out=level_rows.rearrange("(a x) j -> x a j", a=ANCHORS)[x0 : x0 + height],
                     in_=staged[p0 : p0 + height, t],
                 )
 
-        def finish(chunk, queue):
+        def finish(chunk):
             level = chunk["level"]
             if chunk["first_pass"] + chunk["passes"] == level["passes"]:
                 if level["weights_stationary"]:
                     turn_sums(level)
-                decode_and_store(level, queue)
+                decode(level)
 
         for chunk in chunks[:RAW_CHUNKS]:
             load(chunk)
@@ -265,6 +269,9 @@ def tile_head_k_kernel(tc, f0, f1, f2, w0, b0, w1, b1, w2, b2, anchors, out):
             transpose_weights(chunks[step])
             multiply(chunks[step - 1])
             quantise(chunks[step])
-            finish(chunks[step - 1], nc.gpsimd)
+            finish(chunks[step - 1])
+        store(level0)
+        store(level2)
         multiply(chunks[-1])
-        finish(chunks[-1], nc.sync)
+        finish(chunks[-1])
+        store(level1)

@@ -21,8 +21,9 @@ FIELDS = 128
 BANK = 512
 CHUNK_PASSES = 4
 BANK_PASSES = 2
-UNIT_PIXELS = 256
+UNIT_PIXELS = 512
 RUN = 4
+DECODE_STEP = 4
 RAW_CHUNKS = 3
 
 FLOPS = 2 * ANCHORS * FIELDS * IMAGES * (512 * 1024 + 16384 * 256 + 1024 * 64)
@@ -87,20 +88,15 @@ def tile_head_k_kernel(tc, f0, f1, f2, w0, b0, w1, b1, w2, b2, anchors, out):
             w_raw = stream.tile([P, ANCHORS, k1 - k0], BF16, tag="w_raw", bufs=RAW_CHUNKS, name="w_raw")
             nc.sync.dma_start(out=w_raw[:], in_=level["w"][:, k0:k1].rearrange("(a o) k -> o a k", a=ANCHORS))
             chunk["w_raw"] = w_raw
-            chunk["f_raw"] = []
+            f_raw = stream.tile(
+                [P, IMAGES, chunk["passes"], PACK, level["pixels"]], BF16, tag="f_raw", bufs=RAW_CHUNKS, name="f_raw"
+            )
             for n in range(IMAGES):
-                f_raw = stream.tile(
-                    [P, chunk["passes"], PACK, level["pixels"]],
-                    BF16,
-                    tag="f_raw",
-                    bufs=IMAGES * RAW_CHUNKS,
-                    name="f_raw",
-                )
                 nc.sync.dma_start(
-                    out=f_raw[:],
+                    out=f_raw[:, n],
                     in_=level["f"][n, k0:k1].rearrange("(g p t) h w -> p g t (h w)", p=P, t=PACK),
                 )
-                chunk["f_raw"].append(f_raw)
+            chunk["f_raw"] = f_raw
 
         def transpose_weights(chunk):
             w_words = chunk["w_raw"][:].bitcast(F32).rearrange("o a (g p u) -> o a g u p", p=P, u=2)
@@ -120,21 +116,24 @@ def tile_head_k_kernel(tc, f0, f1, f2, w0, b0, w1, b1, w2, b2, anchors, out):
                 chunk["w_grouped"].append(w_grouped)
 
         def regroup(copy, chunk, unit):
-            g, n, x0, width = unit
-            f_grouped = stream.tile([P, width, PACK], BF16, tag="f_grouped", bufs=8, align_bytes=64, name="f_grouped")
+            g, n0, n1, x0, x1 = unit
+            f_grouped = stream.tile(
+                [P, n1 - n0, x1 - x0, PACK], BF16, tag="f_grouped", bufs=6, align_bytes=64, name="f_grouped"
+            )
             copy(
-                out=f_grouped[:].rearrange("p (c i) t -> p c t i", i=RUN),
-                in_=chunk["f_raw"][n][:, g, :, x0 : x0 + width].rearrange("p t (c i) -> p c t i", i=RUN),
+                out=f_grouped[:].rearrange("p n (c i) t -> p n c t i", i=RUN),
+                in_=chunk["f_raw"][:, n0:n1, g, :, x0:x1].rearrange("p n t (c i) -> p n c t i", i=RUN),
             )
             return f_grouped
 
         def quantise_features(chunk, unit, f_grouped):
-            g, n, x0, width = unit
-            first = n * chunk["level"]["pixels"] + x0
+            g, n0, n1, x0, x1 = unit
+            first = n0 * chunk["level"]["pixels"] + x0
+            width = (n1 - n0) * (x1 - x0)
             nc.vector.quantize_mx(
                 out=chunk["f_codes"][:, g, first : first + width].bitcast(FP8X4),
                 scales=chunk["f_scales"][:, g, first : first + width],
-                in_=f_grouped[:].rearrange("p x t -> p (x t)"),
+                in_=f_grouped[:].rearrange("p n x t -> p (n x t)"),
             )
 
         def quantise(chunk):
@@ -144,12 +143,16 @@ def tile_head_k_kernel(tc, f0, f1, f2, w0, b0, w1, b1, w2, b2, anchors, out):
             chunk["f_scales"] = stream.tile([P, passes, IMAGES * pixels], U8, tag="f_scales", align_bytes=64, name="f_scales")
             chunk["w_codes"] = stream.tile([P, ANCHORS, passes, FIELDS], U32, tag="w_codes", align_bytes=64, name="w_codes")
             chunk["w_scales"] = stream.tile([P, ANCHORS, passes, FIELDS], U8, tag="w_scales", align_bytes=64, name="w_scales")
-            width = min(pixels, UNIT_PIXELS)
-            units = [(g, n, x0, width) for n in range(IMAGES) for g in range(passes) for x0 in range(0, pixels, width)]
-            split = len(units) // 2
-            scalar_tiles = [regroup(nc.scalar.copy, chunk, unit) for unit in units[split:]]
+            if pixels > UNIT_PIXELS:
+                units = [(0, n, n + 1, x0, x0 + UNIT_PIXELS) for n in range(IMAGES) for x0 in range(0, pixels, UNIT_PIXELS)]
+            elif passes == 1:
+                units = [(0, n, n + 1, 0, pixels) for n in range(IMAGES)]
+            else:
+                units = [(g, 0, IMAGES, 0, pixels) for g in range(passes)]
+            vector_units, scalar_units = units[0::2], units[1::2]
+            scalar_tiles = [regroup(nc.scalar.copy, chunk, unit) for unit in scalar_units]
             waiting = None
-            for unit in units[:split]:
+            for unit in vector_units:
                 f_grouped = regroup(nc.vector.tensor_copy, chunk, unit)
                 if waiting is not None:
                     quantise_features(chunk, waiting[0], waiting[1])
@@ -161,16 +164,16 @@ def tile_head_k_kernel(tc, f0, f1, f2, w0, b0, w1, b1, w2, b2, anchors, out):
                     scales=chunk["w_scales"][:, a].rearrange("p g o -> p (g o)"),
                     in_=chunk["w_grouped"][a][:].rearrange("p g o t -> p (g o t)"),
                 )
-            for unit, f_grouped in zip(units[split:], scalar_tiles):
+            for unit, f_grouped in zip(scalar_units, scalar_tiles):
                 quantise_features(chunk, unit, f_grouped)
 
         def add_bias(level, y, t):
             bias = spread[:, level["index"], 0:outputs].rearrange("p (a j) -> p a j", a=ANCHORS)
             nc.vector.tensor_tensor(out=level["staged"][:, t], in0=y[:], in1=bias, op=ADD)
 
-        def multiply(chunk):
+        def multiply(chunk, images=range(IMAGES)):
             level = chunk["level"]
-            if chunk["first_pass"] == 0:
+            if chunk["first_pass"] == 0 and 0 in images:
                 tiles = IMAGES * level["pixels"] // P
                 level["staged"] = consts.tile([P, tiles, ANCHORS, FIELDS], F32, name="staged%d" % level["index"])
             if level["weights_stationary"]:
@@ -189,7 +192,7 @@ def tile_head_k_kernel(tc, f0, f1, f2, w0, b0, w1, b1, w2, b2, anchors, out):
                             stop=(k_pass == level["passes"] - 1),
                         )
             else:
-                for t in range(IMAGES * level["pixels"] // P):
+                for t in range(images[0] * level["pixels"] // P, (images[-1] + 1) * level["pixels"] // P):
                     y = psum.tile([P, ANCHORS, FIELDS], F32, tag="y", name="y")
                     for a in range(ANCHORS):
                         for g in range(chunk["passes"]):
@@ -253,9 +256,8 @@ def tile_head_k_kernel(tc, f0, f1, f2, w0, b0, w1, b1, w2, b2, anchors, out):
 
         def finish(chunk):
             level = chunk["level"]
-            if chunk["first_pass"] + chunk["passes"] == level["passes"]:
-                if level["weights_stationary"]:
-                    turn_sums(level)
+            if level["weights_stationary"] and chunk["first_pass"] + chunk["passes"] == level["passes"]:
+                turn_sums(level)
                 decode(level)
 
         for chunk in chunks[:RAW_CHUNKS]:
@@ -267,9 +269,17 @@ def tile_head_k_kernel(tc, f0, f1, f2, w0, b0, w1, b1, w2, b2, anchors, out):
             if step + RAW_CHUNKS - 1 < len(chunks):
                 load(chunks[step + RAW_CHUNKS - 1])
             transpose_weights(chunks[step])
-            multiply(chunks[step - 1])
+            if step == 1:
+                multiply(chunks[0], images=(0,))
+            elif step == 2:
+                multiply(chunks[0], images=(1,))
+            if step > 1:
+                multiply(chunks[step - 1])
             quantise(chunks[step])
             finish(chunks[step - 1])
+            if step == DECODE_STEP:
+                decode(level0)
+                decode(level2)
         store(level0)
         store(level2)
         multiply(chunks[-1])

@@ -20,7 +20,9 @@ ANCHORS = 3
 FIELDS = 128
 BANK = 512
 CHUNK_PASSES = 4
-BANK_PASSES = 2
+END_PASSES = CHUNK_PASSES
+BANK_SLOTS = 2
+PIECE_SLOTS = 4
 UNIT_PIXELS = 512
 RUN = 4
 DECODE_STEP = 4
@@ -43,9 +45,9 @@ def tile_head_k_kernel(tc, f0, f1, f2, w0, b0, w1, b1, w2, b2, anchors, out):
         while first_pass < level["passes"]:
             left = level["passes"] - first_pass
             passes = min(CHUNK_PASSES, left)
-            if level["weights_stationary"] and 1 < left <= CHUNK_PASSES:
-                passes = left // 2
-            chunks.append(dict(level=level, first_pass=first_pass, passes=passes))
+            end = level["weights_stationary"] and left == passes
+            groups = [(0, 2), (2, 3), (3, 4)] if end else [(0, passes)]
+            chunks.append(dict(level=level, first_pass=first_pass, passes=passes, end=end, groups=groups))
             first_pass += passes
 
     with ExitStack() as ctx:
@@ -78,6 +80,11 @@ def tile_head_k_kernel(tc, f0, f1, f2, w0, b0, w1, b1, w2, b2, anchors, out):
                 nc.scalar.copy(out=spread[:, i, :], in_=spread_ps[:])
             nc.vector.tensor_scalar(out=four_anchors, in0=four_anchors, scalar1=4.0, scalar2=None, op0=MULT)
 
+        end_codes = consts.tile([P, 1 + END_PASSES * ANCHORS, FIELDS], U32, align_bytes=64)
+        end_scales = consts.tile([P, 1 + END_PASSES * ANCHORS, FIELDS], U8, align_bytes=64)
+        nc.gpsimd.memset(end_codes[:, 0], 0)
+        nc.gpsimd.memset(end_scales[:, 0], 0)
+
         table_warmer = consts.tile([P, 1], F32)
         nc.scalar.activation(out=table_warmer[:], in_=ones[:, 0:1], func=SIGMOID)
 
@@ -91,29 +98,37 @@ def tile_head_k_kernel(tc, f0, f1, f2, w0, b0, w1, b1, w2, b2, anchors, out):
             f_raw = stream.tile(
                 [P, IMAGES, chunk["passes"], PACK, level["pixels"]], BF16, tag="f_raw", bufs=RAW_CHUNKS, name="f_raw"
             )
-            for n in range(IMAGES):
-                nc.sync.dma_start(
-                    out=f_raw[:, n],
-                    in_=level["f"][n, k0:k1].rearrange("(g p t) h w -> p g t (h w)", p=P, t=PACK),
-                )
+            for g0, g1 in chunk["groups"]:
+                for n in range(IMAGES):
+                    nc.sync.dma_start(
+                        out=f_raw[:, n, g0:g1],
+                        in_=level["f"][n, k0 + g0 * K_PASS : k0 + g1 * K_PASS].rearrange("(g p t) h w -> p g t (h w)", p=P, t=PACK),
+                    )
             chunk["f_raw"] = f_raw
+
+        def slot_of(chunk, g, a):
+            return ANCHORS * g + a if chunk["end"] else chunk["passes"] * a + g
 
         def transpose_weights(chunk):
             w_words = chunk["w_raw"][:].bitcast(F32).rearrange("o a (g p u) -> o a g u p", p=P, u=2)
-            chunk["w_grouped"] = []
-            for a in range(ANCHORS):
-                w_grouped = stream.tile(
-                    [P, chunk["passes"], FIELDS, PACK], BF16, tag="w_grouped", bufs=4, align_bytes=64, name="w_grouped"
-                )
+            slots = {slot_of(chunk, g, a): (g, a) for g in range(chunk["passes"]) for a in range(ANCHORS)}
+            chunk["pieces"] = []
+            first = 0
+            while first < len(slots):
+                left = len(slots) - first
+                count = min(PIECE_SLOTS, left - left % 2 if left > 1 else 1)
+                w_grouped = stream.tile([P, count, FIELDS, PACK], BF16, tag="w_grouped", bufs=6, align_bytes=64, name="w_grouped")
                 grouped_words = w_grouped[:].bitcast(F32)
-                for g0 in range(0, chunk["passes"], BANK_PASSES):
-                    count = min(BANK_PASSES, chunk["passes"] - g0)
-                    w_t = psum.tile([P, count, 2, FIELDS], F32, tag="w_t", name="w_t")
-                    for g in range(count):
+                for s0 in range(0, count, BANK_SLOTS):
+                    s1 = min(s0 + BANK_SLOTS, count)
+                    w_t = psum.tile([P, s1 - s0, 2, FIELDS], F32, tag="w_t", name="w_t")
+                    for s in range(s0, s1):
+                        g, a = slots[first + s]
                         for u in range(2):
-                            nc.tensor.transpose(out=w_t[:, g, u, :], in_=w_words[:, a, g0 + g, u, :], identity=identity[:])
-                    nc.scalar.copy(out=grouped_words[:, g0 : g0 + count], in_=w_t[:].rearrange("p g u o -> p g o u"))
-                chunk["w_grouped"].append(w_grouped)
+                            nc.tensor.transpose(out=w_t[:, s - s0, u, :], in_=w_words[:, a, g, u, :], identity=identity[:])
+                    nc.scalar.copy(out=grouped_words[:, s0:s1], in_=w_t[:].rearrange("p s u o -> p s o u"))
+                chunk["pieces"].append((first, count, w_grouped))
+                first += count
 
         def regroup(copy, chunk, unit):
             g, n0, n1, x0, x1 = unit
@@ -136,17 +151,33 @@ def tile_head_k_kernel(tc, f0, f1, f2, w0, b0, w1, b1, w2, b2, anchors, out):
                 in_=f_grouped[:].rearrange("p n x t -> p (n x t)"),
             )
 
+        def make_codes(chunk):
+            passes = chunk["passes"]
+            columns = IMAGES * chunk["level"]["pixels"]
+            chunk["f_codes"] = stream.tile([P, passes, columns], U32, tag="f_codes", align_bytes=64, name="f_codes")
+            chunk["f_scales"] = stream.tile([P, passes, columns], U8, tag="f_scales", align_bytes=64, name="f_scales")
+            chunk["first_slot"] = 1 if chunk["end"] else 0
+            if chunk["end"]:
+                chunk["w_codes"], chunk["w_scales"] = end_codes, end_scales
+            else:
+                chunk["w_codes"] = stream.tile([P, ANCHORS * passes, FIELDS], U32, tag="w_codes", align_bytes=64, name="w_codes")
+                chunk["w_scales"] = stream.tile([P, ANCHORS * passes, FIELDS], U8, tag="w_scales", align_bytes=64, name="w_scales")
+
+        def quantise_weights(chunk):
+            for first, count, w_grouped in chunk["pieces"]:
+                s0 = chunk["first_slot"] + first
+                nc.vector.quantize_mx(
+                    out=chunk["w_codes"][:, s0 : s0 + count].rearrange("p s o -> p (s o)").bitcast(FP8X4),
+                    scales=chunk["w_scales"][:, s0 : s0 + count].rearrange("p s o -> p (s o)"),
+                    in_=w_grouped[:].rearrange("p s o t -> p (s o t)"),
+                )
+
         def quantise(chunk):
+            make_codes(chunk)
             passes = chunk["passes"]
             pixels = chunk["level"]["pixels"]
-            chunk["f_codes"] = stream.tile([P, passes, IMAGES * pixels], U32, tag="f_codes", align_bytes=64, name="f_codes")
-            chunk["f_scales"] = stream.tile([P, passes, IMAGES * pixels], U8, tag="f_scales", align_bytes=64, name="f_scales")
-            chunk["w_codes"] = stream.tile([P, ANCHORS, passes, FIELDS], U32, tag="w_codes", align_bytes=64, name="w_codes")
-            chunk["w_scales"] = stream.tile([P, ANCHORS, passes, FIELDS], U8, tag="w_scales", align_bytes=64, name="w_scales")
             if pixels > UNIT_PIXELS:
                 units = [(0, n, n + 1, x0, x0 + UNIT_PIXELS) for n in range(IMAGES) for x0 in range(0, pixels, UNIT_PIXELS)]
-            elif passes == 1:
-                units = [(0, n, n + 1, 0, pixels) for n in range(IMAGES)]
             else:
                 units = [(g, 0, IMAGES, 0, pixels) for g in range(passes)]
             vector_units, scalar_units = units[0::2], units[1::2]
@@ -158,12 +189,7 @@ def tile_head_k_kernel(tc, f0, f1, f2, w0, b0, w1, b1, w2, b2, anchors, out):
                     quantise_features(chunk, waiting[0], waiting[1])
                 waiting = (unit, f_grouped)
             quantise_features(chunk, waiting[0], waiting[1])
-            for a in range(ANCHORS):
-                nc.vector.quantize_mx(
-                    out=chunk["w_codes"][:, a].rearrange("p g o -> p (g o)").bitcast(FP8X4),
-                    scales=chunk["w_scales"][:, a].rearrange("p g o -> p (g o)"),
-                    in_=chunk["w_grouped"][a][:].rearrange("p g o t -> p (g o t)"),
-                )
+            quantise_weights(chunk)
             for unit, f_grouped in zip(scalar_units, scalar_tiles):
                 quantise_features(chunk, unit, f_grouped)
 
@@ -182,52 +208,82 @@ def tile_head_k_kernel(tc, f0, f1, f2, w0, b0, w1, b1, w2, b2, anchors, out):
                 for g in range(chunk["passes"]):
                     k_pass = chunk["first_pass"] + g
                     for a in range(ANCHORS):
+                        slot = slot_of(chunk, g, a)
                         nc.tensor.matmul_mx(
                             out=level["sums"][a][:],
-                            lhsT=chunk["w_codes"][:, a, g, :].bitcast(FP8X4),
-                            lhsT_scale=chunk["w_scales"][:, a, g, :],
+                            lhsT=chunk["w_codes"][:, slot, :].bitcast(FP8X4),
+                            lhsT_scale=chunk["w_scales"][:, slot, :],
                             rhs=chunk["f_codes"][:, g, :].bitcast(FP8X4),
                             rhs_scale=chunk["f_scales"][:, g, :],
                             start=(k_pass == 0),
-                            stop=(k_pass == level["passes"] - 1),
+                            stop=(k_pass == level["passes"] - END_PASSES - 1),
                         )
             else:
                 for t in range(images[0] * level["pixels"] // P, (images[-1] + 1) * level["pixels"] // P):
                     y = psum.tile([P, ANCHORS, FIELDS], F32, tag="y", name="y")
                     for a in range(ANCHORS):
                         for g in range(chunk["passes"]):
+                            slot = slot_of(chunk, g, a)
                             nc.tensor.matmul_mx(
                                 out=y[:, a, :],
                                 lhsT=chunk["f_codes"][:, g, t * P : (t + 1) * P].bitcast(FP8X4),
                                 lhsT_scale=chunk["f_scales"][:, g, t * P : (t + 1) * P],
-                                rhs=chunk["w_codes"][:, a, g, :].bitcast(FP8X4),
-                                rhs_scale=chunk["w_scales"][:, a, g, :],
+                                rhs=chunk["w_codes"][:, slot, :].bitcast(FP8X4),
+                                rhs_scale=chunk["w_scales"][:, slot, :],
                                 start=(g == 0),
                                 stop=(g == chunk["passes"] - 1),
                             )
                     add_bias(level, y, t)
 
-        def turn_sums(level):
-            by_field = consts.tile([P, ANCHORS, BANK], F32)
+        def multiply_end(chunk, g):
+            level = chunk["level"]
+            if g == 0:
+                level["ends"] = [psum.tile([P, BANK], F32, tag="y", name="ends%d" % t) for t in range(IMAGES * level["pixels"] // P)]
+            s0 = chunk["first_slot"] + slot_of(chunk, g, 0) - 1
+            s1 = s0 + 1 + ANCHORS
+            for t, ends in enumerate(level["ends"]):
+                nc.tensor.matmul_mx(
+                    out=ends[:],
+                    lhsT=chunk["f_codes"][:, g, t * P : (t + 1) * P].bitcast(FP8X4),
+                    lhsT_scale=chunk["f_scales"][:, g, t * P : (t + 1) * P],
+                    rhs=chunk["w_codes"][:, s0:s1].rearrange("p s o -> p (s o)").bitcast(FP8X4),
+                    rhs_scale=chunk["w_scales"][:, s0:s1].rearrange("p s o -> p (s o)"),
+                    start=(g == 0),
+                    stop=(g == chunk["passes"] - 1),
+                )
+
+        def copy_sums(level):
+            level["by_field"] = consts.tile([P, ANCHORS, BANK], F32, name="by_field")
             for a in range(ANCHORS):
                 copy = nc.vector.tensor_copy if a % 2 else nc.scalar.copy
-                copy(out=by_field[:, a, :], in_=level["sums"][a][:])
+                copy(out=level["by_field"][:, a, :], in_=level["sums"][a][:])
+
+        def turn_sums(level):
             for t in range(IMAGES * level["pixels"] // P):
-                y = psum.tile([P, ANCHORS, FIELDS], F32, tag="y", name="y")
+                y = psum.tile([P, ANCHORS, FIELDS], F32, tag="w_t", name="y")
                 for a in range(ANCHORS):
-                    nc.tensor.transpose(out=y[:, a, :], in_=by_field[:, a, t * P : (t + 1) * P], identity=identity[:])
+                    nc.tensor.transpose(out=y[:, a, :], in_=level["by_field"][:, a, t * P : (t + 1) * P], identity=identity[:])
                 add_bias(level, y, t)
 
-        def decode(level):
+        def sigmoids(level, fields):
+            level["sig"] = consts.tile([P, IMAGES * level["pixels"] // P, ANCHORS, 4], F32, name="sig%d" % level["index"])
+            nc.scalar.activation(
+                out=level["sig"][:].rearrange("p t a s -> p (t a) s"), in_=fields.rearrange("p t a s -> p (t a) s"), func=SIGMOID
+            )
+
+        def decode(level, t0, t1):
             i = level["index"]
-            pixels = level["pixels"]
-            tiles = IMAGES * pixels // P
-            staged = level["staged"]
-            rows = staged[:].rearrange("p t a j -> p (t a) j")
-            sig = consts.tile([P, tiles * ANCHORS, 4], F32, name="sig%d" % i)
-            nc.scalar.activation(out=sig[:], in_=rows[:, :, 0:4], func=SIGMOID)
-            nc.vector.tensor_scalar(out=rows[:, :, 0:2], in0=sig[:, :, 0:2], scalar1=2.0, scalar2=-0.5, op0=MULT, op1=ADD)
-            squares = consts.tile([P, tiles, ANCHORS, 2], F32, name="squares%d" % i)
+            sig = level["sig"][:, t0:t1].rearrange("p t a s -> p (t a) s")
+            staged = level["staged"][:, t0:t1]
+            nc.vector.tensor_scalar(
+                out=staged.rearrange("p t a j -> p (t a) j")[:, :, 0:2],
+                in0=sig[:, :, 0:2],
+                scalar1=2.0,
+                scalar2=-0.5,
+                op0=MULT,
+                op1=ADD,
+            )
+            squares = consts.tile([P, t1 - t0, ANCHORS, 2], F32, name="squares%d_%d" % (i, t0))
             nc.vector.tensor_tensor(
                 out=squares[:].rearrange("p t a s -> p (t a) s"), in0=sig[:, :, 2:4], in1=sig[:, :, 2:4], op=MULT
             )
@@ -237,15 +293,60 @@ def tile_head_k_kernel(tc, f0, f1, f2, w0, b0, w1, b1, w2, b2, anchors, out):
                 in1=four_anchors[:, i, :]
                 .rearrange("p (a s) -> p a s", s=2)
                 .unsqueeze(1)
-                .to_broadcast([P, tiles, ANCHORS, 2]),
+                .to_broadcast([P, t1 - t0, ANCHORS, 2]),
                 op=MULT,
             )
 
-        def store(level):
+        def last_chunk(chunk):
+            level = chunk["level"]
+            pixels = level["pixels"]
+            make_codes(chunk)
+            whole0, whole1 = (0, 0, IMAGES, 0, pixels), (1, 0, IMAGES, 0, pixels)
+            scalar_tile = regroup(nc.scalar.copy, chunk, whole1)
+            vector_tile = regroup(nc.vector.tensor_copy, chunk, whole0)
+            quantise_weights(chunk)
+            quantise_features(chunk, whole0, vector_tile)
+            quantise_features(chunk, whole1, scalar_tile)
+            copy_sums(level)
+            image0, image1 = (2, 0, 1, 0, pixels), (2, 1, 2, 0, pixels)
+            scalar_tile = regroup(nc.scalar.copy, chunk, image1)
+            vector_tile = regroup(nc.vector.tensor_copy, chunk, image0)
+            turn_sums(level)
+            quantise_features(chunk, image0, vector_tile)
+            quantise_features(chunk, image1, scalar_tile)
+            for g in range(3):
+                multiply_end(chunk, g)
+            half = pixels // 2
+            image0, first_half, second_half = (3, 0, 1, 0, pixels), (3, 1, 2, 0, half), (3, 1, 2, half, pixels)
+            scalar_tile = regroup(nc.scalar.copy, chunk, second_half)
+            vector_tiles = [regroup(nc.vector.tensor_copy, chunk, unit) for unit in (image0, first_half)]
+            quantise_features(chunk, image0, vector_tiles[0])
+            quantise_features(chunk, first_half, vector_tiles[1])
+            quantise_features(chunk, second_half, scalar_tile)
+            multiply_end(chunk, 3)
+
+        def finish_level1():
+            level = level1
+            staged = level["staged"]
+            heads = consts.tile([P, len(level["ends"]), ANCHORS, 4], F32)
+            views = [ends[:, FIELDS:].rearrange("p (a j) -> p a j", a=ANCHORS) for ends in level["ends"]]
+            for t, y in enumerate(views):
+                nc.vector.tensor_tensor(out=heads[:, t], in0=y[:, :, 0:4], in1=staged[:, t, :, 0:4], op=ADD)
+            sigmoids(level, heads[:])
+            tiles = len(views) // IMAGES
+            for n in range(IMAGES):
+                for t in range(n * tiles, (n + 1) * tiles):
+                    nc.vector.tensor_tensor(
+                        out=staged[:, t, :, 4:], in0=views[t][:, :, 4:], in1=staged[:, t, :, 4:], op=ADD
+                    )
+                decode(level, n * tiles, (n + 1) * tiles)
+                store(level, [n])
+
+        def store(level, images=range(IMAGES)):
             pixels = level["pixels"]
             staged = level["staged"]
             height = min(P, pixels)
-            for first in range(0, IMAGES * pixels, height):
+            for first in range(images[0] * pixels, (images[-1] + 1) * pixels, height):
                 n, x0 = divmod(first, pixels)
                 t, p0 = divmod(first, P)
                 level_rows = out[n, level["first_row"] : level["first_row"] + ANCHORS * pixels, :]
@@ -253,12 +354,6 @@ def tile_head_k_kernel(tc, f0, f1, f2, w0, b0, w1, b1, w2, b2, anchors, out):
                     out=level_rows.rearrange("(a x) j -> x a j", a=ANCHORS)[x0 : x0 + height],
                     in_=staged[p0 : p0 + height, t],
                 )
-
-        def finish(chunk):
-            level = chunk["level"]
-            if level["weights_stationary"] and chunk["first_pass"] + chunk["passes"] == level["passes"]:
-                turn_sums(level)
-                decode(level)
 
         for chunk in chunks[:RAW_CHUNKS]:
             load(chunk)
@@ -275,13 +370,13 @@ def tile_head_k_kernel(tc, f0, f1, f2, w0, b0, w1, b1, w2, b2, anchors, out):
                 multiply(chunks[0], images=(1,))
             if step > 1:
                 multiply(chunks[step - 1])
-            quantise(chunks[step])
-            finish(chunks[step - 1])
+            if not chunks[step]["end"]:
+                quantise(chunks[step])
             if step == DECODE_STEP:
-                decode(level0)
-                decode(level2)
+                for level in (level0, level2):
+                    sigmoids(level, level["staged"][:, :, :, 0:4])
+                    decode(level, 0, IMAGES * level["pixels"] // P)
         store(level0)
         store(level2)
-        multiply(chunks[-1])
-        finish(chunks[-1])
-        store(level1)
+        last_chunk(chunks[-1])
+        finish_level1()

@@ -34,9 +34,9 @@ FLOPS = 2 * ANCHORS * FIELDS * IMAGES * (512 * 1024 + 16384 * 256 + 1024 * 64)
 def tile_head_k_kernel(tc, f0, f1, f2, w0, b0, w1, b1, w2, b2, anchors, out):
     nc = tc.nc
 
-    level0 = dict(index=0, f=f0, w=w0, first_row=0, weights_stationary=False)
-    level1 = dict(index=1, f=f1, w=w1, first_row=3072, weights_stationary=True)
-    level2 = dict(index=2, f=f2, w=w2, first_row=3840, weights_stationary=False)
+    level0 = dict(index=0, f=f0, w=w0, first_row=0, neighbours=RUN, weights_stationary=False)
+    level1 = dict(index=1, f=f1, w=w1, first_row=3072, neighbours=1, weights_stationary=True)
+    level2 = dict(index=2, f=f2, w=w2, first_row=3840, neighbours=1, weights_stationary=False)
     chunks = []
     for level in (level0, level2, level1):
         level["pixels"] = level["f"].shape[2] * level["f"].shape[3]
@@ -135,8 +135,9 @@ def tile_head_k_kernel(tc, f0, f1, f2, w0, b0, w1, b1, w2, b2, anchors, out):
             f_grouped = stream.tile(
                 [P, n1 - n0, x1 - x0, PACK], BF16, tag="f_grouped", bufs=6, align_bytes=64, name="f_grouped"
             )
+            order = "p n (c i) t -> p n c t i" if chunk["level"]["neighbours"] == 1 else "p n (i c) t -> p n c t i"
             copy(
-                out=f_grouped[:].rearrange("p n (c i) t -> p n c t i", i=RUN),
+                out=f_grouped[:].rearrange(order, i=RUN),
                 in_=chunk["f_raw"][:, n0:n1, g, :, x0:x1].rearrange("p n t (c i) -> p n c t i", i=RUN),
             )
             return f_grouped
@@ -193,15 +194,24 @@ def tile_head_k_kernel(tc, f0, f1, f2, w0, b0, w1, b1, w2, b2, anchors, out):
             for unit, f_grouped in zip(scalar_units, scalar_tiles):
                 quantise_features(chunk, unit, f_grouped)
 
+        def make_staged(level):
+            groups = IMAGES * level["pixels"] // P // level["neighbours"]
+            level["staged"] = consts.tile(
+                [P, groups, ANCHORS, level["neighbours"], FIELDS], F32, name="staged%d" % level["index"]
+            )
+
+        def staged_tile(level, t):
+            group, i = divmod(t, level["neighbours"])
+            return level["staged"][:, group, :, i, :]
+
         def add_bias(level, y, t):
             bias = spread[:, level["index"], 0:outputs].rearrange("p (a j) -> p a j", a=ANCHORS)
-            nc.vector.tensor_tensor(out=level["staged"][:, t], in0=y[:], in1=bias, op=ADD)
+            nc.vector.tensor_tensor(out=staged_tile(level, t), in0=y[:], in1=bias, op=ADD)
 
         def multiply(chunk, images=range(IMAGES)):
             level = chunk["level"]
             if chunk["first_pass"] == 0 and 0 in images:
-                tiles = IMAGES * level["pixels"] // P
-                level["staged"] = consts.tile([P, tiles, ANCHORS, FIELDS], F32, name="staged%d" % level["index"])
+                make_staged(level)
             if level["weights_stationary"]:
                 if chunk["first_pass"] == 0:
                     level["sums"] = [psum.tile([P, BANK], F32, tag="y", name="sums%d" % a) for a in range(ANCHORS)]
@@ -266,36 +276,37 @@ def tile_head_k_kernel(tc, f0, f1, f2, w0, b0, w1, b1, w2, b2, anchors, out):
                 add_bias(level, y, t)
 
         def sigmoids(level, fields):
-            level["sig"] = consts.tile([P, IMAGES * level["pixels"] // P, ANCHORS, 4], F32, name="sig%d" % level["index"])
-            nc.scalar.activation(
-                out=level["sig"][:].rearrange("p t a s -> p (t a) s"), in_=fields.rearrange("p t a s -> p (t a) s"), func=SIGMOID
-            )
+            groups = IMAGES * level["pixels"] // P // level["neighbours"]
+            level["sig"] = consts.tile([P, groups, ANCHORS, level["neighbours"], 4], F32, name="sig%d" % level["index"])
+            order = "p g a i s -> p (g a i) s"
+            nc.scalar.activation(out=level["sig"][:].rearrange(order), in_=fields.rearrange(order), func=SIGMOID)
 
-        def decode(level, t0, t1):
-            i = level["index"]
-            sig = level["sig"][:, t0:t1].rearrange("p t a s -> p (t a) s")
-            staged = level["staged"][:, t0:t1]
+        def decode(level, g0, g1):
+            index = level["index"]
+            order = "p g a i s -> p (g a i) s"
+            sig = level["sig"][:, g0:g1].rearrange(order)
+            staged = level["staged"][:, g0:g1]
             nc.vector.tensor_scalar(
-                out=staged.rearrange("p t a j -> p (t a) j")[:, :, 0:2],
-                in0=sig[:, :, 0:2],
-                scalar1=2.0,
-                scalar2=-0.5,
-                op0=MULT,
-                op1=ADD,
+                out=staged.rearrange(order)[:, :, 0:2], in0=sig[:, :, 0:2], scalar1=2.0, scalar2=-0.5, op0=MULT, op1=ADD
             )
-            squares = consts.tile([P, t1 - t0, ANCHORS, 2], F32, name="squares%d_%d" % (i, t0))
-            nc.vector.tensor_tensor(
-                out=squares[:].rearrange("p t a s -> p (t a) s"), in0=sig[:, :, 2:4], in1=sig[:, :, 2:4], op=MULT
-            )
-            nc.vector.tensor_tensor(
-                out=staged[:, :, :, 2:4],
-                in0=squares[:],
-                in1=four_anchors[:, i, :]
-                .rearrange("p (a s) -> p a s", s=2)
-                .unsqueeze(1)
-                .to_broadcast([P, t1 - t0, ANCHORS, 2]),
-                op=MULT,
-            )
+            squares = consts.tile([P, g1 - g0, ANCHORS, level["neighbours"], 2], F32, name="squares%d_%d" % (index, g0))
+            nc.vector.tensor_tensor(out=squares[:].rearrange(order), in0=sig[:, :, 2:4], in1=sig[:, :, 2:4], op=MULT)
+            scale = four_anchors[:, index, :].rearrange("p (a s) -> p a s", s=2)
+            if level["neighbours"] == 1:
+                nc.vector.tensor_tensor(
+                    out=staged[:, :, :, 0, 2:4],
+                    in0=squares[:, :, :, 0, :],
+                    in1=scale.unsqueeze(1).to_broadcast([P, g1 - g0, ANCHORS, 2]),
+                    op=MULT,
+                )
+            else:
+                for g in range(g1 - g0):
+                    nc.vector.tensor_tensor(
+                        out=staged[:, g, :, :, 2:4],
+                        in0=squares[:, g],
+                        in1=scale.unsqueeze(2).to_broadcast([P, ANCHORS, level["neighbours"], 2]),
+                        op=MULT,
+                    )
 
         def last_chunk(chunk):
             level = chunk["level"]
@@ -327,32 +338,33 @@ def tile_head_k_kernel(tc, f0, f1, f2, w0, b0, w1, b1, w2, b2, anchors, out):
 
         def finish_level1():
             level = level1
-            staged = level["staged"]
-            heads = consts.tile([P, len(level["ends"]), ANCHORS, 4], F32)
+            heads = consts.tile([P, len(level["ends"]), ANCHORS, 1, 4], F32)
             views = [ends[:, FIELDS:].rearrange("p (a j) -> p a j", a=ANCHORS) for ends in level["ends"]]
             for t, y in enumerate(views):
-                nc.vector.tensor_tensor(out=heads[:, t], in0=y[:, :, 0:4], in1=staged[:, t, :, 0:4], op=ADD)
+                nc.vector.tensor_tensor(
+                    out=heads[:, t, :, 0, :], in0=y[:, :, 0:4], in1=staged_tile(level, t)[:, :, 0:4], op=ADD
+                )
             sigmoids(level, heads[:])
             tiles = len(views) // IMAGES
             for n in range(IMAGES):
                 for t in range(n * tiles, (n + 1) * tiles):
-                    nc.vector.tensor_tensor(
-                        out=staged[:, t, :, 4:], in0=views[t][:, :, 4:], in1=staged[:, t, :, 4:], op=ADD
-                    )
+                    staged = staged_tile(level, t)[:, :, 4:]
+                    nc.vector.tensor_tensor(out=staged, in0=views[t][:, :, 4:], in1=staged, op=ADD)
                 decode(level, n * tiles, (n + 1) * tiles)
                 store(level, [n])
 
         def store(level, images=range(IMAGES)):
             pixels = level["pixels"]
-            staged = level["staged"]
+            neighbours = level["neighbours"]
             height = min(P, pixels)
-            for first in range(images[0] * pixels, (images[-1] + 1) * pixels, height):
+            for first in range(images[0] * pixels, (images[-1] + 1) * pixels, height * neighbours):
                 n, x0 = divmod(first, pixels)
-                t, p0 = divmod(first, P)
+                group, p0 = divmod(first // neighbours, P)
                 level_rows = out[n, level["first_row"] : level["first_row"] + ANCHORS * pixels, :]
+                q0 = x0 // neighbours
                 nc.sync.dma_start(
-                    out=level_rows.rearrange("(a x) j -> x a j", a=ANCHORS)[x0 : x0 + height],
-                    in_=staged[p0 : p0 + height, t],
+                    out=level_rows.rearrange("(a q i) j -> q a (i j)", a=ANCHORS, i=neighbours)[q0 : q0 + height],
+                    in_=level["staged"][p0 : p0 + height, group].rearrange("p a i j -> p a (i j)"),
                 )
 
         for chunk in chunks[:RAW_CHUNKS]:
@@ -374,8 +386,8 @@ def tile_head_k_kernel(tc, f0, f1, f2, w0, b0, w1, b1, w2, b2, anchors, out):
                 quantise(chunks[step])
             if step == DECODE_STEP:
                 for level in (level0, level2):
-                    sigmoids(level, level["staged"][:, :, :, 0:4])
-                    decode(level, 0, IMAGES * level["pixels"] // P)
+                    sigmoids(level, level["staged"][:, :, :, :, 0:4])
+                    decode(level, 0, IMAGES * level["pixels"] // P // level["neighbours"])
         store(level0)
         store(level2)
         last_chunk(chunks[-1])

@@ -24,6 +24,7 @@ END_PASSES = CHUNK_PASSES
 BANK_SLOTS = 2
 PIECE_SLOTS = 4
 UNIT_PIXELS = 512
+SCALAR_PIXELS = 192
 RUN = 4
 DECODE_STEP = 4
 RAW_CHUNKS = 3
@@ -130,16 +131,21 @@ def tile_head_k_kernel(tc, f0, f1, f2, w0, b0, w1, b1, w2, b2, anchors, out):
                 chunk["pieces"].append((first, count, w_grouped))
                 first += count
 
-        def regroup(copy, chunk, unit):
+        def make_grouped(unit):
             g, n0, n1, x0, x1 = unit
-            f_grouped = stream.tile(
-                [P, n1 - n0, x1 - x0, PACK], BF16, tag="f_grouped", bufs=6, align_bytes=64, name="f_grouped"
-            )
+            return stream.tile([P, n1 - n0, x1 - x0, PACK], BF16, tag="f_grouped", bufs=6, align_bytes=64, name="f_grouped")
+
+        def regroup_part(copy, chunk, unit, f_grouped, p0, p1):
+            g, n0, n1, x0, x1 = unit
             order = "p n (c i) t -> p n c t i" if chunk["level"]["neighbours"] == 1 else "p n (i c) t -> p n c t i"
             copy(
-                out=f_grouped[:].rearrange(order, i=RUN),
-                in_=chunk["f_raw"][:, n0:n1, g, :, x0:x1].rearrange("p n t (c i) -> p n c t i", i=RUN),
+                out=f_grouped[:, :, p0:p1].rearrange(order, i=RUN),
+                in_=chunk["f_raw"][:, n0:n1, g, :, x0 + p0 : x0 + p1].rearrange("p n t (c i) -> p n c t i", i=RUN),
             )
+
+        def regroup(copy, chunk, unit):
+            f_grouped = make_grouped(unit)
+            regroup_part(copy, chunk, unit, f_grouped, 0, unit[4] - unit[3])
             return f_grouped
 
         def quantise_features(chunk, unit, f_grouped):
@@ -182,7 +188,16 @@ def tile_head_k_kernel(tc, f0, f1, f2, w0, b0, w1, b1, w2, b2, anchors, out):
             else:
                 units = [(g, 0, IMAGES, 0, pixels) for g in range(passes)]
             vector_units, scalar_units = units[0::2], units[1::2]
-            scalar_tiles = [regroup(nc.scalar.copy, chunk, unit) for unit in scalar_units]
+            shared = chunk["level"]["weights_stationary"]
+            scalar_tiles = []
+            for i, unit in enumerate(scalar_units):
+                f_grouped = make_grouped(unit)
+                width = unit[4] - unit[3]
+                cut = SCALAR_PIXELS if shared and i == 0 else width
+                regroup_part(nc.scalar.copy, chunk, unit, f_grouped, 0, cut)
+                if cut < width:
+                    regroup_part(nc.vector.tensor_copy, chunk, unit, f_grouped, cut, width)
+                scalar_tiles.append(f_grouped)
             waiting = None
             for unit in vector_units:
                 f_grouped = regroup(nc.vector.tensor_copy, chunk, unit)

@@ -25,7 +25,8 @@ BANK_SLOTS = 2
 PIECE_SLOTS = 4
 UNIT_PIXELS = 512
 SCALAR_PIXELS = 192
-RUN = 4
+RUN = 8
+NEIGHBOURS = 4
 DECODE_STEP = 4
 RAW_CHUNKS = 3
 
@@ -35,7 +36,7 @@ FLOPS = 2 * ANCHORS * FIELDS * IMAGES * (512 * 1024 + 16384 * 256 + 1024 * 64)
 def tile_head_k_kernel(tc, f0, f1, f2, w0, b0, w1, b1, w2, b2, anchors, out):
     nc = tc.nc
 
-    level0 = dict(index=0, f=f0, w=w0, first_row=0, neighbours=RUN, weights_stationary=False)
+    level0 = dict(index=0, f=f0, w=w0, first_row=0, neighbours=NEIGHBOURS, weights_stationary=False)
     level1 = dict(index=1, f=f1, w=w1, first_row=3072, neighbours=1, weights_stationary=True)
     level2 = dict(index=2, f=f2, w=w2, first_row=3840, neighbours=1, weights_stationary=False)
     chunks = []
@@ -137,10 +138,12 @@ def tile_head_k_kernel(tc, f0, f1, f2, w0, b0, w1, b1, w2, b2, anchors, out):
 
         def regroup_part(copy, chunk, unit, f_grouped, p0, p1):
             g, n0, n1, x0, x1 = unit
-            order = "p n (c i) t -> p n c t i" if chunk["level"]["neighbours"] == 1 else "p n (i c) t -> p n c t i"
+            neighbours = chunk["level"]["neighbours"]
+            run = RUN if neighbours == 1 else neighbours
+            order = "p n (c i) t -> p n c t i" if neighbours == 1 else "p n (i c) t -> p n c t i"
             copy(
-                out=f_grouped[:, :, p0:p1].rearrange(order, i=RUN),
-                in_=chunk["f_raw"][:, n0:n1, g, :, x0 + p0 : x0 + p1].rearrange("p n t (c i) -> p n c t i", i=RUN),
+                out=f_grouped[:, :, p0:p1].rearrange(order, i=run),
+                in_=chunk["f_raw"][:, n0:n1, g, :, x0 + p0 : x0 + p1].rearrange("p n t (c i) -> p n c t i", i=run),
             )
 
         def regroup(copy, chunk, unit):

from contextlib import ExitStack

import concourse.mybir as mybir
from concourse.masks import make_identity

BF16 = mybir.dt.bfloat16
F32 = mybir.dt.float32
U32 = mybir.dt.uint32
U8 = mybir.dt.uint8
FP8X4 = mybir.dt.float8_e4m3fn_x4
ADD = mybir.AluOpType.add
MULT = mybir.AluOpType.mult
SIGMOID = mybir.ActivationFunctionType.Sigmoid

P = 128
PACK = 4
K_PASS = P * PACK
IMAGES = 2
ANCHORS = 3
FIELDS = 128
BANK = 512
CHUNK_PASSES = 4
END_PASSES = CHUNK_PASSES
BANK_SLOTS = 2
PIECE_SLOTS = 4
UNIT_PIXELS = 512
SCALAR_PIXELS = 192
RUN = 8
NEIGHBOURS = 4
DECODE_STEP = 4
RAW_CHUNKS = 3

FLOPS = 2 * ANCHORS * FIELDS * IMAGES * (512 * 1024 + 16384 * 256 + 1024 * 64)


def tile_head_k_kernel(tc, f0, f1, f2, w0, b0, w1, b1, w2, b2, anchors, out):
    nc = tc.nc

    level0 = dict(index=0, f=f0, w=w0, first_row=0, neighbours=NEIGHBOURS, weights_stationary=False)
    level1 = dict(index=1, f=f1, w=w1, first_row=3072, neighbours=1, weights_stationary=True)
    level2 = dict(index=2, f=f2, w=w2, first_row=3840, neighbours=1, weights_stationary=False)
    chunks = []
    for level in (level0, level2, level1):
        level["pixels"] = level["f"].shape[2] * level["f"].shape[3]
        level["passes"] = level["w"].shape[1] // K_PASS
        first_pass = 0
        while first_pass < level["passes"]:
            left = level["passes"] - first_pass
            passes = min(CHUNK_PASSES, left)
            end = level["weights_stationary"] and left == passes
            groups = [(0, 2), (2, 3), (3, 4)] if end else [(0, passes)]
            chunks.append(dict(level=level, first_pass=first_pass, passes=passes, end=end, groups=groups))
            first_pass += passes

    with ExitStack() as ctx:
        ctx.enter_context(tc.manual_schedule())
        consts = ctx.enter_context(tc.tile_pool(name="consts", bufs=1))
        stream = ctx.enter_context(tc.tile_pool(name="stream", bufs=2))
        psum = ctx.enter_context(tc.psum_pool(name="psum", bufs=4))

        identity = consts.tile([P, P], F32)
        make_identity(nc, identity[:])

        ones = consts.tile([P, P], BF16)
        nc.vector.memset(ones[:], 1.0)
        row0 = consts.tile([P, 3, BANK], BF16)
        nc.vector.memset(row0[:], 0.0)
        outputs = ANCHORS * FIELDS
        for i, b in enumerate((b0, b1, b2)):
            nc.scalar.dma_start(out=row0[0:1, i, 0:outputs], in_=b.rearrange("(x o) -> x o", x=1))
        nc.scalar.dma_start(
            out=row0[0:1, :, outputs : outputs + 2 * ANCHORS],
            in_=anchors.rearrange("(x l) a s -> x l (a s)", x=1),
        )
        spread = consts.tile([P, 3, BANK], F32)
        four_anchors = spread[:, :, outputs : outputs + 2 * ANCHORS]

        def spread_constants():
            for i in range(3):
                spread_ps = psum.tile([P, BANK], F32, tag="y")
                nc.tensor.matmul(out=spread_ps[:], lhsT=ones[:], rhs=row0[:, i, :], start=True, stop=True)
                nc.scalar.copy(out=spread[:, i, :], in_=spread_ps[:])
            nc.vector.tensor_scalar(out=four_anchors, in0=four_anchors, scalar1=4.0, scalar2=None, op0=MULT)

        end_codes = consts.tile([P, 1 + END_PASSES * ANCHORS, FIELDS], U32, align_bytes=64)
        end_scales = consts.tile([P, 1 + END_PASSES * ANCHORS, FIELDS], U8, align_bytes=64)
        nc.gpsimd.memset(end_codes[:, 0], 0)
        nc.gpsimd.memset(end_scales[:, 0], 0)

        table_warmer = consts.tile([P, 1], F32)
        nc.scalar.activation(out=table_warmer[:], in_=ones[:, 0:1], func=SIGMOID)

        def load(chunk):
            level = chunk["level"]
            k0 = chunk["first_pass"] * K_PASS
            k1 = k0 + chunk["passes"] * K_PASS
            w_raw = stream.tile([P, ANCHORS, k1 - k0], BF16, tag="w_raw", bufs=RAW_CHUNKS, name="w_raw")
            nc.sync.dma_start(out=w_raw[:], in_=level["w"][:, k0:k1].rearrange("(a o) k -> o a k", a=ANCHORS))
            chunk["w_raw"] = w_raw
            f_raw = stream.tile(
                [P, IMAGES, chunk["passes"], PACK, level["pixels"]], BF16, tag="f_raw", bufs=RAW_CHUNKS, name="f_raw"
            )
            for g0, g1 in chunk["groups"]:
                for n in range(IMAGES):
                    nc.sync.dma_start(
                        out=f_raw[:, n, g0:g1],
                        in_=level["f"][n, k0 + g0 * K_PASS : k0 + g1 * K_PASS].rearrange("(g p t) h w -> p g t (h w)", p=P, t=PACK),
                    )
            chunk["f_raw"] = f_raw

        def slot_of(chunk, g, a):
            return ANCHORS * g + a if chunk["end"] else chunk["passes"] * a + g

        def transpose_weights(chunk):
            w_words = chunk["w_raw"][:].bitcast(F32).rearrange("o a (g p u) -> o a g u p", p=P, u=2)
            slots = {slot_of(chunk, g, a): (g, a) for g in range(chunk["passes"]) for a in range(ANCHORS)}
            chunk["pieces"] = []
            first = 0
            while first < len(slots):
                left = len(slots) - first
                count = min(PIECE_SLOTS, left - left % 2 if left > 1 else 1)
                w_grouped = stream.tile([P, count, FIELDS, PACK], BF16, tag="w_grouped", bufs=6, align_bytes=64, name="w_grouped")
                grouped_words = w_grouped[:].bitcast(F32)
                for s0 in range(0, count, BANK_SLOTS):
                    s1 = min(s0 + BANK_SLOTS, count)
                    w_t = psum.tile([P, s1 - s0, 2, FIELDS], F32, tag="w_t", name="w_t")
                    for s in range(s0, s1):
                        g, a = slots[first + s]
                        for u in range(2):
                            nc.tensor.transpose(out=w_t[:, s - s0, u, :], in_=w_words[:, a, g, u, :], identity=identity[:])
                    nc.scalar.copy(out=grouped_words[:, s0:s1], in_=w_t[:].rearrange("p s u o -> p s o u"))
                chunk["pieces"].append((first, count, w_grouped))
                first += count

        def make_grouped(unit):
            g, n0, n1, x0, x1 = unit
            return stream.tile([P, n1 - n0, x1 - x0, PACK], BF16, tag="f_grouped", bufs=6, align_bytes=64, name="f_grouped")

        def regroup_part(copy, chunk, unit, f_grouped, p0, p1):
            g, n0, n1, x0, x1 = unit
            neighbours = chunk["level"]["neighbours"]
            run = RUN if neighbours == 1 else neighbours
            order = "p n (c i) t -> p n c t i" if neighbours == 1 else "p n (i c) t -> p n c t i"
            copy(
                out=f_grouped[:, :, p0:p1].rearrange(order, i=run),
                in_=chunk["f_raw"][:, n0:n1, g, :, x0 + p0 : x0 + p1].rearrange("p n t (c i) -> p n c t i", i=run),
            )

        def regroup(copy, chunk, unit):
            f_grouped = make_grouped(unit)
            regroup_part(copy, chunk, unit, f_grouped, 0, unit[4] - unit[3])
            return f_grouped

        def quantise_features(chunk, unit, f_grouped):
            g, n0, n1, x0, x1 = unit
            first = n0 * chunk["level"]["pixels"] + x0
            width = (n1 - n0) * (x1 - x0)
            nc.vector.quantize_mx(
                out=chunk["f_codes"][:, g, first : first + width].bitcast(FP8X4),
                scales=chunk["f_scales"][:, g, first : first + width],
                in_=f_grouped[:].rearrange("p n x t -> p (n x t)"),
            )

        def make_codes(chunk):
            passes = chunk["passes"]
            columns = IMAGES * chunk["level"]["pixels"]
            chunk["f_codes"] = stream.tile([P, passes, columns], U32, tag="f_codes", align_bytes=64, name="f_codes")
            chunk["f_scales"] = stream.tile([P, passes, columns], U8, tag="f_scales", align_bytes=64, name="f_scales")
            chunk["first_slot"] = 1 if chunk["end"] else 0
            if chunk["end"]:
                chunk["w_codes"], chunk["w_scales"] = end_codes, end_scales
            else:
                chunk["w_codes"] = stream.tile([P, ANCHORS * passes, FIELDS], U32, tag="w_codes", align_bytes=64, name="w_codes")
                chunk["w_scales"] = stream.tile([P, ANCHORS * passes, FIELDS], U8, tag="w_scales", align_bytes=64, name="w_scales")

        def quantise_weights(chunk):
            for first, count, w_grouped in chunk["pieces"]:
                s0 = chunk["first_slot"] + first
                nc.vector.quantize_mx(
                    out=chunk["w_codes"][:, s0 : s0 + count].rearrange("p s o -> p (s o)").bitcast(FP8X4),
                    scales=chunk["w_scales"][:, s0 : s0 + count].rearrange("p s o -> p (s o)"),
                    in_=w_grouped[:].rearrange("p s o t -> p (s o t)"),
                )

        def quantise(chunk):
            make_codes(chunk)
            passes = chunk["passes"]
            pixels = chunk["level"]["pixels"]
            if pixels > UNIT_PIXELS:
                units = [(0, n, n + 1, x0, x0 + UNIT_PIXELS) for n in range(IMAGES) for x0 in range(0, pixels, UNIT_PIXELS)]
            else:
                units = [(g, 0, IMAGES, 0, pixels) for g in range(passes)]
            vector_units, scalar_units = units[0::2], units[1::2]
            shared = chunk["level"]["weights_stationary"]
            scalar_tiles = []
            for i, unit in enumerate(scalar_units):
                f_grouped = make_grouped(unit)
                width = unit[4] - unit[3]
                cut = SCALAR_PIXELS if shared and i == 0 else width
                regroup_part(nc.scalar.copy, chunk, unit, f_grouped, 0, cut)
                if cut < width:
                    regroup_part(nc.vector.tensor_copy, chunk, unit, f_grouped, cut, width)
                scalar_tiles.append(f_grouped)
            waiting = None
            for unit in vector_units:
                f_grouped = regroup(nc.vector.tensor_copy, chunk, unit)
                if waiting is not None:
                    quantise_features(chunk, waiting[0], waiting[1])
                waiting = (unit, f_grouped)
            quantise_features(chunk, waiting[0], waiting[1])
            quantise_weights(chunk)
            for unit, f_grouped in zip(scalar_units, scalar_tiles):
                quantise_features(chunk, unit, f_grouped)

        def make_staged(level):
            groups = IMAGES * level["pixels"] // P // level["neighbours"]
            level["staged"] = consts.tile(
                [P, groups, ANCHORS, level["neighbours"], FIELDS], F32, name="staged%d" % level["index"]
            )

        def staged_tile(level, t):
            group, i = divmod(t, level["neighbours"])
            return level["staged"][:, group, :, i, :]

        def add_bias(level, y, t):
            bias = spread[:, level["index"], 0:outputs].rearrange("p (a j) -> p a j", a=ANCHORS)
            nc.vector.tensor_tensor(out=staged_tile(level, t), in0=y[:], in1=bias, op=ADD)

        def multiply(chunk, images=range(IMAGES)):
            level = chunk["level"]
            if chunk["first_pass"] == 0 and 0 in images:
                make_staged(level)
            if level["weights_stationary"]:
                if chunk["first_pass"] == 0:
                    level["sums"] = [psum.tile([P, BANK], F32, tag="y", name="sums%d" % a) for a in range(ANCHORS)]
                for g in range(chunk["passes"]):
                    k_pass = chunk["first_pass"] + g
                    for a in range(ANCHORS):
                        slot = slot_of(chunk, g, a)
                        nc.tensor.matmul_mx(
                            out=level["sums"][a][:],
                            lhsT=chunk["w_codes"][:, slot, :].bitcast(FP8X4),
                            lhsT_scale=chunk["w_scales"][:, slot, :],
                            rhs=chunk["f_codes"][:, g, :].bitcast(FP8X4),
                            rhs_scale=chunk["f_scales"][:, g, :],
                            start=(k_pass == 0),
                            stop=(k_pass == level["passes"] - END_PASSES - 1),
                        )
            else:
                for t in range(images[0] * level["pixels"] // P, (images[-1] + 1) * level["pixels"] // P):
                    y = psum.tile([P, ANCHORS, FIELDS], F32, tag="y", name="y")
                    for a in range(ANCHORS):
                        for g in range(chunk["passes"]):
                            slot = slot_of(chunk, g, a)
                            nc.tensor.matmul_mx(
                                out=y[:, a, :],
                                lhsT=chunk["f_codes"][:, g, t * P : (t + 1) * P].bitcast(FP8X4),
                                lhsT_scale=chunk["f_scales"][:, g, t * P : (t + 1) * P],
                                rhs=chunk["w_codes"][:, slot, :].bitcast(FP8X4),
                                rhs_scale=chunk["w_scales"][:, slot, :],
                                start=(g == 0),
                                stop=(g == chunk["passes"] - 1),
                            )
                    add_bias(level, y, t)

        def multiply_end(chunk, g):
            level = chunk["level"]
            if g == 0:
                level["ends"] = [psum.tile([P, BANK], F32, tag="y", name="ends%d" % t) for t in range(IMAGES * level["pixels"] // P)]
            s0 = chunk["first_slot"] + slot_of(chunk, g, 0) - 1
            s1 = s0 + 1 + ANCHORS
            for t, ends in enumerate(level["ends"]):
                nc.tensor.matmul_mx(
                    out=ends[:],
                    lhsT=chunk["f_codes"][:, g, t * P : (t + 1) * P].bitcast(FP8X4),
                    lhsT_scale=chunk["f_scales"][:, g, t * P : (t + 1) * P],
                    rhs=chunk["w_codes"][:, s0:s1].rearrange("p s o -> p (s o)").bitcast(FP8X4),
                    rhs_scale=chunk["w_scales"][:, s0:s1].rearrange("p s o -> p (s o)"),
                    start=(g == 0),
                    stop=(g == chunk["passes"] - 1),
                )

        def copy_sums(level):
            level["by_field"] = consts.tile([P, ANCHORS, BANK], F32, name="by_field")
            for a in range(ANCHORS):
                copy = nc.vector.tensor_copy if a % 2 else nc.scalar.copy
                copy(out=level["by_field"][:, a, :], in_=level["sums"][a][:])

        def turn_sums(level):
            for t in range(IMAGES * level["pixels"] // P):
                y = psum.tile([P, ANCHORS, FIELDS], F32, tag="w_t", name="y")
                for a in range(ANCHORS):
                    nc.tensor.transpose(out=y[:, a, :], in_=level["by_field"][:, a, t * P : (t + 1) * P], identity=identity[:])
                add_bias(level, y, t)

        def sigmoids(level, fields):
            groups = IMAGES * level["pixels"] // P // level["neighbours"]
            level["sig"] = consts.tile([P, groups, ANCHORS, level["neighbours"], 4], F32, name="sig%d" % level["index"])
            order = "p g a i s -> p (g a i) s"
            nc.scalar.activation(out=level["sig"][:].rearrange(order), in_=fields.rearrange(order), func=SIGMOID)

        def decode(level, g0, g1):
            index = level["index"]
            order = "p g a i s -> p (g a i) s"
            sig = level["sig"][:, g0:g1].rearrange(order)
            staged = level["staged"][:, g0:g1]
            nc.vector.tensor_scalar(
                out=staged.rearrange(order)[:, :, 0:2], in0=sig[:, :, 0:2], scalar1=2.0, scalar2=-0.5, op0=MULT, op1=ADD
            )
            squares = consts.tile([P, g1 - g0, ANCHORS, level["neighbours"], 2], F32, name="squares%d_%d" % (index, g0))
            nc.vector.tensor_tensor(out=squares[:].rearrange(order), in0=sig[:, :, 2:4], in1=sig[:, :, 2:4], op=MULT)
            scale = four_anchors[:, index, :].rearrange("p (a s) -> p a s", s=2)
            if level["neighbours"] == 1:
                nc.vector.tensor_tensor(
                    out=staged[:, :, :, 0, 2:4],
                    in0=squares[:, :, :, 0, :],
                    in1=scale.unsqueeze(1).to_broadcast([P, g1 - g0, ANCHORS, 2]),
                    op=MULT,
                )
            else:
                for g in range(g1 - g0):
                    nc.vector.tensor_tensor(
                        out=staged[:, g, :, :, 2:4],
                        in0=squares[:, g],
                        in1=scale.unsqueeze(2).to_broadcast([P, ANCHORS, level["neighbours"], 2]),
                        op=MULT,
                    )

        def last_chunk(chunk):
            level = chunk["level"]
            pixels = level["pixels"]
            make_codes(chunk)
            whole0, whole1 = (0, 0, IMAGES, 0, pixels), (1, 0, IMAGES, 0, pixels)
            scalar_tile = regroup(nc.scalar.copy, chunk, whole1)
            vector_tile = regroup(nc.vector.tensor_copy, chunk, whole0)
            quantise_weights(chunk)
            quantise_features(chunk, whole0, vector_tile)
            quantise_features(chunk, whole1, scalar_tile)
            copy_sums(level)
            image0, image1 = (2, 0, 1, 0, pixels), (2, 1, 2, 0, pixels)
            scalar_tile = regroup(nc.scalar.copy, chunk, image1)
            vector_tile = regroup(nc.vector.tensor_copy, chunk, image0)
            turn_sums(level)
            quantise_features(chunk, image0, vector_tile)
            quantise_features(chunk, image1, scalar_tile)
            for g in range(3):
                multiply_end(chunk, g)
            half = pixels // 2
            image0, first_half, second_half = (3, 0, 1, 0, pixels), (3, 1, 2, 0, half), (3, 1, 2, half, pixels)
            scalar_tile = regroup(nc.scalar.copy, chunk, second_half)
            vector_tiles = [regroup(nc.vector.tensor_copy, chunk, unit) for unit in (image0, first_half)]
            quantise_features(chunk, image0, vector_tiles[0])
            quantise_features(chunk, first_half, vector_tiles[1])
            quantise_features(chunk, second_half, scalar_tile)
            multiply_end(chunk, 3)

        def finish_level1():
            level = level1
            heads = consts.tile([P, len(level["ends"]), ANCHORS, 1, 4], F32)
            views = [ends[:, FIELDS:].rearrange("p (a j) -> p a j", a=ANCHORS) for ends in level["ends"]]
            for t, y in enumerate(views):
                nc.vector.tensor_tensor(
                    out=heads[:, t, :, 0, :], in0=y[:, :, 0:4], in1=staged_tile(level, t)[:, :, 0:4], op=ADD
                )
            sigmoids(level, heads[:])
            tiles = len(views) // IMAGES
            for n in range(IMAGES):
                for t in range(n * tiles, (n + 1) * tiles):
                    staged = staged_tile(level, t)[:, :, 4:]
                    nc.vector.tensor_tensor(out=staged, in0=views[t][:, :, 4:], in1=staged, op=ADD)
                decode(level, n * tiles, (n + 1) * tiles)
                store(level, [n])

        def store(level, images=range(IMAGES)):
            pixels = level["pixels"]
            neighbours = level["neighbours"]
            height = min(P, pixels)
            for first in range(images[0] * pixels, (images[-1] + 1) * pixels, height * neighbours):
                n, x0 = divmod(first, pixels)
                group, p0 = divmod(first // neighbours, P)
                level_rows = out[n, level["first_row"] : level["first_row"] + ANCHORS * pixels, :]
                q0 = x0 // neighbours
                nc.sync.dma_start(
                    out=level_rows.rearrange("(a q i) j -> q a (i j)", a=ANCHORS, i=neighbours)[q0 : q0 + height],
                    in_=level["staged"][p0 : p0 + height, group].rearrange("p a i j -> p a (i j)"),
                )

        for chunk in chunks[:RAW_CHUNKS]:
            load(chunk)
        transpose_weights(chunks[0])
        quantise(chunks[0])
        spread_constants()
        for step in range(1, len(chunks)):
            if step + RAW_CHUNKS - 1 < len(chunks):
                load(chunks[step + RAW_CHUNKS - 1])
            transpose_weights(chunks[step])
            if step == 1:
                multiply(chunks[0], images=(0,))
            elif step == 2:
                multiply(chunks[0], images=(1,))
            if step > 1:
                multiply(chunks[step - 1])
            if not chunks[step]["end"]:
                quantise(chunks[step])
            if step == DECODE_STEP:
                for level in (level0, level2):
                    sigmoids(level, level["staged"][:, :, :, :, 0:4])
                    decode(level, 0, IMAGES * level["pixels"] // P // level["neighbours"])
        store(level0)
        store(level2)
        last_chunk(chunks[-1])
        finish_level1()
